import numpy as np
import ml_dtypes


def mxq(x, axis, fmt="e4m3"):
    dtype, down = {"e4m3": (ml_dtypes.float8_e4m3fn, 7), "e5m2": (ml_dtypes.float8_e5m2, 14)}[fmt]
    v = np.moveaxis(np.asarray(x, np.float32).astype(ml_dtypes.bfloat16).astype(np.float64), axis, -1)
    blocks = v.reshape(v.shape[:-1] + (-1, 32))
    amax = np.abs(blocks).max(-1, keepdims=True)
    byte = np.maximum(np.where(amax > 0, np.frexp(amax)[1] - 1 + 127, 0) - down, 1)
    scale = np.exp2(byte - 127.0)
    codes = (blocks / scale).astype(np.float32).astype(dtype).astype(np.float64)
    return np.moveaxis((codes * scale).reshape(v.shape), -1, axis)


WIDE = False


def mx_kscale(k):
    if not WIDE:
        return np.ones(k)
    levels = np.array([10, -10, 5, -5, 0])
    a = np.random.permutation(np.resize(levels, k // 512 * 4)).reshape(k // 512, 4)
    idx = np.arange(k)
    return np.exp2(a[idx // 512, idx % 128 // 32])


BF16 = ml_dtypes.bfloat16


def bf(x):
    return np.asarray(x, np.float32).astype(BF16)


def f64(x):
    return np.asarray(x).astype(np.float64)


B, D, H, F, C, R = 1024, 4096, 1024, 1024, 128, 32
P_FACTOR = 3.0
RHO = 0.75
P_LABEL = 0.1


def unit_rows(x):
    return x / np.sqrt((x ** 2).sum(-1, keepdims=True))


def setup_inputs():
    s = mx_kscale(F)
    u = np.exp2(np.round(np.log2(mx_kscale(D)) / P_FACTOR))
    basis = np.random.standard_normal((R, F))
    off = np.random.standard_normal(F) * 0.1
    f = np.random.standard_normal((B, R)) @ basis * np.sqrt(RHO / R) + np.sqrt(1.0 - RHO) * np.random.standard_normal((B, F)) + off
    e = np.random.standard_normal((D, R)) @ basis * np.sqrt(RHO / R) + np.sqrt(1.0 - RHO) * np.random.standard_normal((D, F)) + off
    return {"f_n": bf(unit_rows(f) * s),
            "ex_n": bf(unit_rows(e) / s * u[:, None]),
            "ex_classes": bf((np.random.uniform(size=(D, C)) < P_LABEL) / (u * u * u)[:, None]),
            "class_reps": bf(np.eye(C) + np.random.standard_normal((C, C)) / np.sqrt(C))}


def reference(f_n, ex_n, ex_classes, class_reps):
    s = mxq(f64(f_n), 1, "e4m3") @ mxq(f64(ex_n), 1, "e4m3").T
    a = np.sign(s) * np.abs(s) ** P_FACTOR
    ex_class_reps = f64(ex_classes) @ f64(class_reps)
    echo = mxq(a, 1, "e4m3") @ mxq(ex_class_reps, 0, "e4m3")
    d2 = np.stack([((echo - r) ** 2).sum(-1) for r in f64(class_reps)], axis=1)
    return -np.sqrt(d2)

@@ -1,0 +1,327 @@
+from contextlib import ExitStack
+
+import concourse.mybir as mybir
+from concourse.masks import make_identity
+
+F32 = mybir.dt.float32
+BF16 = mybir.dt.bfloat16
+U32 = mybir.dt.uint32
+U8 = mybir.dt.uint8
+FP8X4 = mybir.dt.float8_e4m3fn_x4
+ACT = mybir.ActivationFunctionType
+ALU = mybir.AluOpType
+
+P = 128
+B, D, F, C = 1024, 4096, 1024, 128
+FLOPS = 2 * B * D * F + 2 * D * C * C + 2 * B * D * C + 4 * B * C * C
+
+RING = 6
+
+
+def tile_minerva_detex_pb_kernel(tc, f_n, ex_n, ex_classes, class_reps, out):
+    nc = tc.nc
+    with ExitStack() as ctx:
+        ctx.enter_context(tc.manual_schedule())
+        const = ctx.enter_context(tc.tile_pool(name="const", bufs=1))
+        loads = ctx.enter_context(tc.tile_pool(name="loads", bufs=1))
+        keep = ctx.enter_context(tc.tile_pool(name="keep", bufs=1))
+        grouped_pool = ctx.enter_context(tc.tile_pool(name="grouped", bufs=4))
+        xcodes_pool = ctx.enter_context(tc.tile_pool(name="xcodes", bufs=3))
+        sq_pool = ctx.enter_context(tc.tile_pool(name="sq", bufs=3))
+        a_pool = ctx.enter_context(tc.tile_pool(name="a", bufs=3))
+        acodes_pool = ctx.enter_context(tc.tile_pool(name="acodes", bufs=4))
+        c_pool = ctx.enter_context(tc.tile_pool(name="c", bufs=2))
+        tail = ctx.enter_context(tc.tile_pool(name="tail", bufs=2))
+        psum = ctx.enter_context(tc.psum_pool(name="psum", bufs=1))
+
+        ex_v = ex_n.rearrange("(g p j) f -> p g j f", p=P, j=4)
+        f_v = f_n.rearrange("(p t) f -> p t f", t=8)
+        exc_v = ex_classes.rearrange("(g p j) c -> p g j c", p=P, j=4)
+        out_v = out.rearrange("(p t) k -> p t k", t=8)
+
+        ident_f = const.tile([P, P], F32, name="ident_f")
+        make_identity(nc, ident_f[:])
+        ident_b = const.tile([P, P], BF16, name="ident_b")
+        make_identity(nc, ident_b[:])
+        warm = const.tile([P, 1], F32, name="warm")
+        nc.vector.memset(warm[:], 1.0)
+        warm_out = const.tile([P, 1], F32, name="warm_out")
+        nc.scalar.activation(out=warm_out[:], in_=warm[:], func=ACT.Sqrt)
+        ones_f = const.tile([P, P], F32, name="ones_f")
+        nc.vector.memset(ones_f[:], 1.0)
+
+        ex_rows = {}
+        for j in range(4):
+            t = loads.tile([P, F], BF16, name="ex0_%d" % j)
+            nc.sync.dma_start(out=t[:], in_=ex_v[:, 0, j, :])
+            ex_rows[(0, j)] = t[:]
+        f_rows = {}
+        for bt in range(4):
+            t = loads.tile([P, F], BF16, name="f_%d" % bt)
+            nc.sync.dma_start(out=t[:], in_=f_v[:, bt, :])
+            f_rows[bt] = t[:]
+        f_hi = loads.tile([P, 4, F], BF16, name="f_hi")
+        nc.sync.dma_start(out=f_hi[:], in_=f_v[:, 4:8, :])
+        for bt in range(4, 8):
+            f_rows[bt] = f_hi[:, bt - 4, :]
+        reps = const.tile([P, C], BF16, name="reps")
+        exc_sb = loads.tile([P, 8, 4, C], BF16, name="exc_sb")
+        for g in range(1, 8):
+            t = loads.tile([P, 4, F], BF16, name="ex%d" % g)
+            nc.sync.dma_start(out=t[:], in_=ex_v[:, g, :, :])
+            for j in range(4):
+                ex_rows[(g, j)] = t[:, j, :]
+            if g == 1:
+                nc.sync.dma_start(out=reps[:], in_=class_reps)
+                nc.sync.dma_start(out=exc_sb[:], in_=exc_v)
+
+        echo = [psum.tile([P, 512], F32, name="echo%d" % h) for h in range(2)]
+        banks = []
+
+        def ring_bank(dtype):
+            i = len(banks)
+            bank = psum.tile([P, 512], dtype, tag="ring%d" % (i % RING), name="bank%d" % i)
+            banks.append(bank)
+            return bank
+
+        def copy_out(engine, out_ap, in_ap):
+            if engine == "scalar":
+                nc.scalar.copy(out=out_ap, in_=in_ap)
+            else:
+                nc.vector.tensor_copy(out=out_ap, in_=in_ap)
+
+        def transpose_rows(rows, dst, engine):
+            bank = ring_bank(F32)
+            words = rows.bitcast(F32)
+            for i in range(4):
+                nc.tensor.transpose(bank[:, i * P : (i + 1) * P], words[:, i * P : (i + 1) * P], ident_f[:])
+            copy_out(
+                engine,
+                dst.bitcast(F32).rearrange("p (kp r u) -> p kp r u", kp=2, u=2),
+                bank[:].rearrange("p (kp u r) -> p kp r u", kp=2, u=2),
+            )
+
+        def quantise(src, codes, scales):
+            nc.vector.quantize_mx(out=codes.bitcast(FP8X4), scales=scales, in_=src)
+
+        ex_codes = {}
+        pair_tiles = {}
+
+        def ex_pair(v, engines):
+            g, hh = divmod(v, 2)
+            if hh == 0:
+                xc = xcodes_pool.tile([P, 1024], U32, tag="xc", name="xc%d" % g, align_bytes=64)
+                xs = xcodes_pool.tile([P, 1024], U8, tag="xs", name="xs%d" % g, align_bytes=64)
+                ex_codes[g] = (xc, xs)
+            grp = grouped_pool.tile([P, 2, F], BF16, tag="grouped", name="xg%d" % v, align_bytes=64)
+            for jj in range(2):
+                transpose_rows(ex_rows[(g, 2 * hh + jj)], grp[:, jj, :], engines[jj])
+            pair_tiles[v] = grp
+
+        def quantise_ex_pair(v):
+            g, hh = divmod(v, 2)
+            xc, xs = ex_codes[g]
+            cols = slice(hh * 512, (hh + 1) * 512)
+            quantise(pair_tiles[v][:].rearrange("p a b -> p (a b)"), xc[:, cols], xs[:, cols])
+
+        f_codes = {}
+        f_tiles = {}
+
+        def f_tile(bt, engine):
+            i, jj = divmod(bt, 2)
+            if jj == 0:
+                f_tiles[i] = grouped_pool.tile([P, 2, F], BF16, tag="grouped", name="fg%d" % i, align_bytes=64)
+            transpose_rows(f_rows[bt], f_tiles[i][:, jj, :], engine)
+
+        def quantise_f_pair(i):
+            fc = keep.tile([P, 512], U32, name="fc%d" % i, align_bytes=64)
+            fs = keep.tile([P, 512], U8, name="fs%d" % i, align_bytes=64)
+            f_codes[i] = (fc, fs)
+            quantise(f_tiles[i][:].rearrange("p a b -> p (a b)"), fc[:], fs[:])
+
+        a_tiles = {}
+        a_codes = {}
+
+        def s_bank(n):
+            g, bt = divmod(n, 8)
+            u, i = divmod(n, 4)
+            bank = ring_bank(F32)
+            xc, xs = ex_codes[g]
+            fc, fs = f_codes[bt // 2]
+            for j in range(4):
+                for kp in range(2):
+                    lc = slice((2 * j + kp) * P, (2 * j + kp + 1) * P)
+                    rc = slice((2 * (bt % 2) + kp) * P, (2 * (bt % 2) + kp + 1) * P)
+                    nc.tensor.matmul_mx(
+                        out=bank[:, j * P : (j + 1) * P],
+                        lhsT=xc[:, lc].bitcast(FP8X4),
+                        lhsT_scale=xs[:, lc],
+                        rhs=fc[:, rc].bitcast(FP8X4),
+                        rhs_scale=fs[:, rc],
+                        start=(kp == 0),
+                        stop=(kp == 1),
+                    )
+            by_query = bank[:].rearrange("p (j b) -> p b j", j=4)
+            sq = sq_pool.tile([P, P, 4], F32, tag="sq", name="sq%d" % n)
+            nc.scalar.activation(out=sq[:], in_=by_query, func=ACT.Square)
+            if i == 0:
+                a_tiles[u] = a_pool.tile([P, 4, P, 4], BF16, tag="a", name="a%d" % u, align_bytes=64)
+            nc.vector.tensor_tensor(out=a_tiles[u][:, i, :, :], in0=sq[:], in1=by_query, op=ALU.mult)
+
+        def quantise_a(u):
+            ac = acodes_pool.tile([P, 512], U32, tag="ac", name="ac%d" % u, align_bytes=64)
+            asc = acodes_pool.tile([P, 512], U8, tag="as", name="as%d" % u, align_bytes=64)
+            a_codes[u] = (ac, asc)
+            quantise(a_tiles[u][:].rearrange("p i b j -> p (i b j)"), ac[:], asc[:])
+
+        ct_tiles = {}
+        c_codes = {}
+
+        def classes_transpose(g):
+            bank = ring_bank(BF16)
+            for j in range(4):
+                nc.tensor.transpose(bank[:, j * P : (j + 1) * P], exc_sb[:, g, j, :], ident_b[:])
+            ct = c_pool.tile([P, 512], BF16, tag="ct", name="ct%d" % g)
+            nc.scalar.copy(out=ct[:], in_=bank[:])
+            ct_tiles[g] = ct
+
+        def class_reps_of_exemplars(g):
+            bank = ring_bank(F32)
+            for j in range(4):
+                nc.tensor.matmul(
+                    bank[:, j * P : (j + 1) * P],
+                    lhsT=ct_tiles[g][:, j * P : (j + 1) * P],
+                    rhs=reps[:],
+                    start=True,
+                    stop=True,
+                )
+            cg = c_pool.tile([P, 512], BF16, tag="cg", name="cg%d" % g, align_bytes=64)
+            nc.scalar.copy(
+                out=cg[:].rearrange("p (c j) -> p c j", j=4), in_=bank[:].rearrange("p (j c) -> p c j", j=4)
+            )
+            cc = keep.tile([P, P], U32, name="cc%d" % g, align_bytes=64)
+            cs = keep.tile([P, P], U8, name="cs%d" % g, align_bytes=64)
+            c_codes[g] = (cc, cs)
+            quantise(cg[:], cc[:], cs[:])
+
+        def echo_pass(u):
+            g, h = divmod(u, 2)
+            cc, cs = c_codes[g]
+            ac, asc = a_codes[u]
+            nc.tensor.matmul_mx(
+                out=echo[h][:],
+                lhsT=cc[:].bitcast(FP8X4),
+                lhsT_scale=cs[:],
+                rhs=ac[:].bitcast(FP8X4),
+                rhs_scale=asc[:],
+                start=(g == 0),
+                stop=(g == 7),
+            )
+
+        reps_t2 = const.tile([P, C], F32, name="reps_t2")
+        reps_tsq = const.tile([P, C], F32, name="reps_tsq")
+        rr = const.tile([P, C], F32, name="rr")
+
+        def reps_transpose():
+            bank = ring_bank(BF16)
+            nc.tensor.transpose(bank[:, 0:P], reps[:], ident_b[:])
+            nc.scalar.mul(out=reps_t2[:], in_=bank[:, 0:P], mul=-2.0)
+            nc.scalar.activation(out=reps_tsq[:], in_=bank[:, 0:P], func=ACT.Square)
+
+        def reps_norms():
+            bank = ring_bank(F32)
+            nc.tensor.matmul(bank[:, 0:P], lhsT=ones_f[:], rhs=reps_tsq[:], start=True, stop=True)
+            nc.vector.tensor_copy(out=rr[:], in_=bank[:, 0:P])
+
+        e_tiles = {}
+
+        def echo_out(h):
+            et = tail.tile([P, 512], F32, tag="et", name="et%d" % h)
+            e2t = tail.tile([P, 512], F32, tag="e2t", name="e2t%d" % h)
+            for i in range(4):
+                cols = slice(i * P, (i + 1) * P)
+                nc.scalar.copy(out=et[:, cols], in_=echo[h][:, cols])
+                nc.scalar.activation(out=e2t[:, cols], in_=echo[h][:, cols], func=ACT.Square)
+            e_tiles[h] = (et, e2t)
+
+        def distances(h):
+            et, e2t = e_tiles[h]
+            o = tail.tile([P, 4, C], F32, tag="o", name="o%d" % h)
+            for c in range(2):
+                bank = ring_bank(F32)
+                for i2 in range(2):
+                    cols = slice((2 * c + i2) * P, (2 * c + i2 + 1) * P)
+                    dst = bank[:, i2 * P : (i2 + 1) * P]
+                    nc.tensor.matmul(dst, lhsT=et[:, cols], rhs=reps_t2[:], start=True, stop=False)
+                    nc.tensor.matmul(dst, lhsT=e2t[:, cols], rhs=ones_f[:], start=False, stop=True)
+                d2 = tail.tile([P, 2, C], F32, tag="d2", name="d2_%d%d" % (h, c))
+                nc.vector.tensor_tensor(
+                    out=d2[:],
+                    in0=bank[:, 0 : 2 * P].rearrange("p (i k) -> p i k", i=2),
+                    in1=rr[:].unsqueeze(1).to_broadcast([P, 2, C]),
+                    op=ALU.add,
+                )
+                nc.vector.tensor_scalar_max(out=d2[:], in0=d2[:], scalar1=0.0)
+                dist = tail.tile([P, 2, C], F32, tag="dist", name="dist%d%d" % (h, c))
+                nc.scalar.activation(out=dist[:], in_=d2[:], func=ACT.Sqrt)
+                nc.vector.tensor_scalar_mul(out=o[:, 2 * c : 2 * c + 2, :], in0=dist[:], scalar1=-1.0)
+            nc.sync.dma_start(out=out_v[:, 4 * h : 4 * h + 4, :], in_=o[:])
+
+        ex_pair(0, ("scalar", "vector"))
+        ex_pair(1, ("scalar", "vector"))
+        quantise_ex_pair(0)
+        f_tile(0, "scalar")
+        f_tile(1, "vector")
+        quantise_ex_pair(1)
+        f_tile(2, "scalar")
+        quantise_f_pair(0)
+        f_tile(3, "vector")
+        quantise_f_pair(1)
+        for n in range(64):
+            u, i = divmod(n, 4)
+            g, h = divmod(u, 2)
+            if n == 2:
+                f_tile(4, "scalar")
+                f_tile(5, "vector")
+                quantise_f_pair(2)
+            if n == 3:
+                f_tile(6, "scalar")
+                f_tile(7, "vector")
+                quantise_f_pair(3)
+            if n == 5:
+                ex_pair(2, ("scalar", "scalar"))
+                quantise_ex_pair(2)
+            if n == 7:
+                ex_pair(3, ("scalar", "scalar"))
+                classes_transpose(0)
+                classes_transpose(1)
+                reps_transpose()
+                quantise_ex_pair(3)
+            if n == 9:
+                class_reps_of_exemplars(0)
+                reps_norms()
+            if i == 0 and u >= 2:
+                if u + 2 < 16:
+                    ex_pair(u + 2, ("scalar", "scalar"))
+                if h == 1 and g + 1 < 8:
+                    classes_transpose(g + 1)
+                if u + 2 < 16:
+                    quantise_ex_pair(u + 2)
+            if i == 1 and h == 0 and g >= 1:
+                class_reps_of_exemplars(g)
+            if i == 3:
+                if u == 3:
+                    echo_pass(0)
+                    echo_pass(1)
+                    echo_pass(2)
+                elif u > 3:
+                    echo_pass(u - 1)
+                if u == 15:
+                    echo_out(0)
+            s_bank(n)
+            if i == 3:
+                quantise_a(u)
+        distances(0)
+        echo_pass(15)
+        echo_out(1)
+        distances(1)

@@ -29,8 +29,8 @@ def tile_minerva_detex_pb_kernel(tc, f_n, ex_n, ex_classes, class_reps, out):
         xcodes_pool = ctx.enter_context(tc.tile_pool(name="xcodes", bufs=3))
         sq_pool = ctx.enter_context(tc.tile_pool(name="sq", bufs=3))
         a_pool = ctx.enter_context(tc.tile_pool(name="a", bufs=3))
-        acodes_pool = ctx.enter_context(tc.tile_pool(name="acodes", bufs=4))
-        c_pool = ctx.enter_context(tc.tile_pool(name="c", bufs=2))
+        acodes_pool = ctx.enter_context(tc.tile_pool(name="acodes", bufs=6))
+        c_pool = ctx.enter_context(tc.tile_pool(name="c", bufs=3))
         tail = ctx.enter_context(tc.tile_pool(name="tail", bufs=2))
         psum = ctx.enter_context(tc.psum_pool(name="psum", bufs=1))
 
@@ -71,7 +71,7 @@ def tile_minerva_detex_pb_kernel(tc, f_n, ex_n, ex_classes, class_reps, out):
             nc.sync.dma_start(out=t[:], in_=ex_v[:, g, :, :])
             for j in range(4):
                 ex_rows[(g, j)] = t[:, j, :]
-            if g == 1:
+            if g == 2:
                 nc.sync.dma_start(out=reps[:], in_=class_reps)
                 nc.sync.dma_start(out=exc_sb[:], in_=exc_v)
 
@@ -109,10 +109,6 @@ def tile_minerva_detex_pb_kernel(tc, f_n, ex_n, ex_classes, class_reps, out):
 
         def ex_pair(v, engines):
             g, hh = divmod(v, 2)
-            if hh == 0:
-                xc = xcodes_pool.tile([P, 1024], U32, tag="xc", name="xc%d" % g, align_bytes=64)
-                xs = xcodes_pool.tile([P, 1024], U8, tag="xs", name="xs%d" % g, align_bytes=64)
-                ex_codes[g] = (xc, xs)
             grp = grouped_pool.tile([P, 2, F], BF16, tag="grouped", name="xg%d" % v, align_bytes=64)
             for jj in range(2):
                 transpose_rows(ex_rows[(g, 2 * hh + jj)], grp[:, jj, :], engines[jj])
@@ -120,24 +116,23 @@ def tile_minerva_detex_pb_kernel(tc, f_n, ex_n, ex_classes, class_reps, out):
 
         def quantise_ex_pair(v):
             g, hh = divmod(v, 2)
+            if hh == 0:
+                xc = xcodes_pool.tile([P, 1024], U32, tag="xc", name="xc%d" % g, align_bytes=64)
+                xs = xcodes_pool.tile([P, 1024], U8, tag="xs", name="xs%d" % g, align_bytes=64)
+                ex_codes[g] = (xc, xs)
             xc, xs = ex_codes[g]
             cols = slice(hh * 512, (hh + 1) * 512)
             quantise(pair_tiles[v][:].rearrange("p a b -> p (a b)"), xc[:, cols], xs[:, cols])
 
         f_codes = {}
-        f_tiles = {}
 
-        def f_tile(bt, engine):
-            i, jj = divmod(bt, 2)
-            if jj == 0:
-                f_tiles[i] = grouped_pool.tile([P, 2, F], BF16, tag="grouped", name="fg%d" % i, align_bytes=64)
-            transpose_rows(f_rows[bt], f_tiles[i][:, jj, :], engine)
-
-        def quantise_f_pair(i):
-            fc = keep.tile([P, 512], U32, name="fc%d" % i, align_bytes=64)
-            fs = keep.tile([P, 512], U8, name="fs%d" % i, align_bytes=64)
-            f_codes[i] = (fc, fs)
-            quantise(f_tiles[i][:].rearrange("p a b -> p (a b)"), fc[:], fs[:])
+        def f_tile(bt):
+            fg = grouped_pool.tile([P, F], BF16, tag="fgrouped", name="fg%d" % bt, align_bytes=64)
+            transpose_rows(f_rows[bt], fg[:], "scalar")
+            fc = keep.tile([P, 256], U32, name="fc%d" % bt, align_bytes=64)
+            fs = keep.tile([P, 256], U8, name="fs%d" % bt, align_bytes=64)
+            f_codes[bt] = (fc, fs)
+            quantise(fg[:], fc[:], fs[:])
 
         a_tiles = {}
         a_codes = {}
@@ -147,11 +142,11 @@ def tile_minerva_detex_pb_kernel(tc, f_n, ex_n, ex_classes, class_reps, out):
             u, i = divmod(n, 4)
             bank = ring_bank(F32)
             xc, xs = ex_codes[g]
-            fc, fs = f_codes[bt // 2]
+            fc, fs = f_codes[bt]
             for j in range(4):
                 for kp in range(2):
                     lc = slice((2 * j + kp) * P, (2 * j + kp + 1) * P)
-                    rc = slice((2 * (bt % 2) + kp) * P, (2 * (bt % 2) + kp + 1) * P)
+                    rc = slice(kp * P, (kp + 1) * P)
                     nc.tensor.matmul_mx(
                         out=bank[:, j * P : (j + 1) * P],
                         lhsT=xc[:, lc].bitcast(FP8X4),
@@ -175,6 +170,7 @@ def tile_minerva_detex_pb_kernel(tc, f_n, ex_n, ex_classes, class_reps, out):
             quantise(a_tiles[u][:].rearrange("p i b j -> p (i b j)"), ac[:], asc[:])
 
         ct_tiles = {}
+        cg_tiles = {}
         c_codes = {}
 
         def classes_transpose(g):
@@ -199,10 +195,13 @@ def tile_minerva_detex_pb_kernel(tc, f_n, ex_n, ex_classes, class_reps, out):
             nc.scalar.copy(
                 out=cg[:].rearrange("p (c j) -> p c j", j=4), in_=bank[:].rearrange("p (j c) -> p c j", j=4)
             )
+            cg_tiles[g] = cg
+
+        def quantise_class_reps(g):
             cc = keep.tile([P, P], U32, name="cc%d" % g, align_bytes=64)
             cs = keep.tile([P, P], U8, name="cs%d" % g, align_bytes=64)
             c_codes[g] = (cc, cs)
-            quantise(cg[:], cc[:], cs[:])
+            quantise(cg_tiles[g][:], cc[:], cs[:])
 
         def echo_pass(u):
             g, h = divmod(u, 2)
@@ -234,6 +233,9 @@ def tile_minerva_detex_pb_kernel(tc, f_n, ex_n, ex_classes, class_reps, out):
             nc.vector.tensor_copy(out=rr[:], in_=bank[:, 0:P])
 
         e_tiles = {}
+        d_banks = {}
+        d2_tiles = {}
+        o_tiles = {}
 
         def echo_out(h):
             et = tail.tile([P, 512], F32, tag="et", name="et%d" % h)
@@ -243,85 +245,107 @@ def tile_minerva_detex_pb_kernel(tc, f_n, ex_n, ex_classes, class_reps, out):
                 nc.scalar.copy(out=et[:, cols], in_=echo[h][:, cols])
                 nc.scalar.activation(out=e2t[:, cols], in_=echo[h][:, cols], func=ACT.Square)
             e_tiles[h] = (et, e2t)
+            o_tiles[h] = tail.tile([P, 4, C], F32, tag="o", name="o%d" % h)
 
-        def distances(h):
+        def distance_products(h, c):
             et, e2t = e_tiles[h]
-            o = tail.tile([P, 4, C], F32, tag="o", name="o%d" % h)
-            for c in range(2):
-                bank = ring_bank(F32)
-                for i2 in range(2):
-                    cols = slice((2 * c + i2) * P, (2 * c + i2 + 1) * P)
-                    dst = bank[:, i2 * P : (i2 + 1) * P]
-                    nc.tensor.matmul(dst, lhsT=et[:, cols], rhs=reps_t2[:], start=True, stop=False)
-                    nc.tensor.matmul(dst, lhsT=e2t[:, cols], rhs=ones_f[:], start=False, stop=True)
-                d2 = tail.tile([P, 2, C], F32, tag="d2", name="d2_%d%d" % (h, c))
-                nc.vector.tensor_tensor(
-                    out=d2[:],
-                    in0=bank[:, 0 : 2 * P].rearrange("p (i k) -> p i k", i=2),
-                    in1=rr[:].unsqueeze(1).to_broadcast([P, 2, C]),
-                    op=ALU.add,
-                )
-                nc.vector.tensor_scalar_max(out=d2[:], in0=d2[:], scalar1=0.0)
-                dist = tail.tile([P, 2, C], F32, tag="dist", name="dist%d%d" % (h, c))
-                nc.scalar.activation(out=dist[:], in_=d2[:], func=ACT.Sqrt)
-                nc.vector.tensor_scalar_mul(out=o[:, 2 * c : 2 * c + 2, :], in0=dist[:], scalar1=-1.0)
-            nc.sync.dma_start(out=out_v[:, 4 * h : 4 * h + 4, :], in_=o[:])
+            bank = ring_bank(F32)
+            for i2 in range(2):
+                cols = slice((2 * c + i2) * P, (2 * c + i2 + 1) * P)
+                dst = bank[:, i2 * P : (i2 + 1) * P]
+                nc.tensor.matmul(dst, lhsT=et[:, cols], rhs=reps_t2[:], start=True, stop=False)
+                nc.tensor.matmul(dst, lhsT=e2t[:, cols], rhs=ones_f[:], start=False, stop=True)
+            d_banks[(h, c)] = bank
 
-        ex_pair(0, ("scalar", "vector"))
-        ex_pair(1, ("scalar", "vector"))
+        def distance_sum(h, c):
+            d2 = tail.tile([P, 2, C], F32, tag="d2", name="d2_%d%d" % (h, c))
+            nc.vector.tensor_tensor(
+                out=d2[:],
+                in0=d_banks[(h, c)][:, 0 : 2 * P].rearrange("p (i k) -> p i k", i=2),
+                in1=rr[:].unsqueeze(1).to_broadcast([P, 2, C]),
+                op=ALU.add,
+            )
+            d2_tiles[(h, c)] = d2
+
+        def distance_root(h, c):
+            d2 = d2_tiles[(h, c)]
+            nc.scalar.activation(out=d2[:], in_=d2[:], func=ACT.Relu)
+            nc.scalar.activation(out=d2[:], in_=d2[:], func=ACT.Sqrt)
+            nc.scalar.mul(out=o_tiles[h][:, 2 * c : 2 * c + 2, :], in_=d2[:], mul=-1.0)
+
+        def store(h):
+            nc.sync.dma_start(out=out_v[:, 4 * h : 4 * h + 4, :], in_=o_tiles[h][:])
+
+        both_scalar = ("scalar", "scalar")
+        ex_pair(0, both_scalar)
         quantise_ex_pair(0)
-        f_tile(0, "scalar")
-        f_tile(1, "vector")
+        ex_pair(1, both_scalar)
         quantise_ex_pair(1)
-        f_tile(2, "scalar")
-        quantise_f_pair(0)
-        f_tile(3, "vector")
-        quantise_f_pair(1)
-        for n in range(64):
-            u, i = divmod(n, 4)
+        for bt in range(4):
+            f_tile(bt)
+        quantised = [2]
+        for u in range(16):
             g, h = divmod(u, 2)
-            if n == 2:
-                f_tile(4, "scalar")
-                f_tile(5, "vector")
-                quantise_f_pair(2)
-            if n == 3:
-                f_tile(6, "scalar")
-                f_tile(7, "vector")
-                quantise_f_pair(3)
-            if n == 5:
-                ex_pair(2, ("scalar", "scalar"))
-                quantise_ex_pair(2)
-            if n == 7:
-                ex_pair(3, ("scalar", "scalar"))
+            if u == 2:
+                ex_pair(4, ("scalar", "vector"))
+                ex_pair(5, ("scalar", "vector"))
+            elif u >= 3 and u + 3 < 16:
+                ex_pair(u + 3, both_scalar)
+            if u == 3:
                 classes_transpose(0)
                 classes_transpose(1)
                 reps_transpose()
-                quantise_ex_pair(3)
-            if n == 9:
-                class_reps_of_exemplars(0)
-                reps_norms()
-            if i == 0 and u >= 2:
-                if u + 2 < 16:
-                    ex_pair(u + 2, ("scalar", "scalar"))
-                if h == 1 and g + 1 < 8:
-                    classes_transpose(g + 1)
-                if u + 2 < 16:
-                    quantise_ex_pair(u + 2)
-            if i == 1 and h == 0 and g >= 1:
-                class_reps_of_exemplars(g)
-            if i == 3:
-                if u == 3:
-                    echo_pass(0)
-                    echo_pass(1)
-                    echo_pass(2)
-                elif u > 3:
-                    echo_pass(u - 1)
-                if u == 15:
-                    echo_out(0)
-            s_bank(n)
-            if i == 3:
-                quantise_a(u)
-        distances(0)
+            if h == 1 and u >= 3 and g + 1 < 8:
+                classes_transpose(g + 1)
+            if u >= 3:
+                for v in range(quantised[0], min(u + 3, 16)):
+                    quantise_ex_pair(v)
+                quantised[0] = min(u + 3, 16)
+            if u >= 1:
+                quantise_a(u - 1)
+            if h == 0 and g >= 2:
+                quantise_class_reps(g)
+            for i in range(4):
+                n = 4 * u + i
+                if n == 2:
+                    for bt in range(4, 8):
+                        f_tile(bt)
+                if n == 4:
+                    ex_pair(2, both_scalar)
+                if n == 6:
+                    ex_pair(3, both_scalar)
+                    quantise_ex_pair(2)
+                    quantise_ex_pair(3)
+                    quantised[0] = 4
+                if n == 17:
+                    class_reps_of_exemplars(0)
+                    class_reps_of_exemplars(1)
+                    reps_norms()
+                    quantise_class_reps(0)
+                    quantise_class_reps(1)
+                if i == 1:
+                    if u == 5:
+                        for uu in range(4):
+                            echo_pass(uu)
+                    elif u > 5:
+                        echo_pass(u - 2)
+                s_bank(n)
+            if h == 1 and u >= 3 and g + 1 < 8:
+                class_reps_of_exemplars(g + 1)
+        echo_pass(14)
+        echo_out(0)
+        distance_products(0, 0)
+        distance_products(0, 1)
+        distance_sum(0, 0)
+        quantise_a(15)
         echo_pass(15)
+        distance_root(0, 0)
+        distance_sum(0, 1)
         echo_out(1)
-        distances(1)
+        distance_root(0, 1)
+        store(0)
+        for c in range(2):
+            distance_products(1, c)
+            distance_sum(1, c)
+            distance_root(1, c)
+        store(1)

@@ -126,13 +126,18 @@ def tile_minerva_detex_pb_kernel(tc, f_n, ex_n, ex_classes, class_reps, out):
 
         f_codes = {}
 
-        def f_tile(bt):
+        f_tiles = {}
+
+        def f_transpose(bt, engine):
             fg = grouped_pool.tile([P, F], BF16, tag="fgrouped", name="fg%d" % bt, align_bytes=64)
-            transpose_rows(f_rows[bt], fg[:], "scalar")
+            transpose_rows(f_rows[bt], fg[:], engine)
+            f_tiles[bt] = fg
+
+        def quantise_f(bt):
             fc = keep.tile([P, 256], U32, name="fc%d" % bt, align_bytes=64)
             fs = keep.tile([P, 256], U8, name="fs%d" % bt, align_bytes=64)
             f_codes[bt] = (fc, fs)
-            quantise(fg[:], fc[:], fs[:])
+            quantise(f_tiles[bt][:], fc[:], fs[:])
 
         a_tiles = {}
         a_codes = {}
@@ -282,7 +287,8 @@ def tile_minerva_detex_pb_kernel(tc, f_n, ex_n, ex_classes, class_reps, out):
         ex_pair(1, both_scalar)
         quantise_ex_pair(1)
         for bt in range(4):
-            f_tile(bt)
+            f_transpose(bt, "scalar")
+            quantise_f(bt)
         quantised = [2]
         for u in range(16):
             g, h = divmod(u, 2)
@@ -307,9 +313,11 @@ def tile_minerva_detex_pb_kernel(tc, f_n, ex_n, ex_classes, class_reps, out):
                 quantise_class_reps(g)
             for i in range(4):
                 n = 4 * u + i
-                if n == 2:
+                if n == 3:
                     for bt in range(4, 8):
-                        f_tile(bt)
+                        f_transpose(bt, ("scalar", "vector")[bt % 2])
+                    for bt in range(4, 8):
+                        quantise_f(bt)
                 if n == 4:
                     ex_pair(2, both_scalar)
                 if n == 6:
@@ -341,11 +349,28 @@ def tile_minerva_detex_pb_kernel(tc, f_n, ex_n, ex_classes, class_reps, out):
         echo_pass(15)
         distance_root(0, 0)
         distance_sum(0, 1)
-        echo_out(1)
+        et = tail.tile([P, 512], F32, tag="et", name="et1")
+        e2t = tail.tile([P, 512], F32, tag="e2t", name="e2t1")
+        o = tail.tile([P, 4, C], F32, tag="o", name="o1")
+        for i in range(4):
+            cols = slice(i * P, (i + 1) * P)
+            nc.scalar.copy(out=et[:, cols], in_=echo[1][:, cols])
+            nc.vector.tensor_tensor(out=e2t[:, cols], in0=et[:, cols], in1=et[:, cols], op=ALU.mult)
         distance_root(0, 1)
         store(0)
-        for c in range(2):
-            distance_products(1, c)
-            distance_sum(1, c)
-            distance_root(1, c)
-        store(1)
+        roots = []
+        for i in range(4):
+            cols = slice(i * P, (i + 1) * P)
+            bank = ring_bank(F32)
+            nc.tensor.matmul(bank[:, 0:P], lhsT=et[:, cols], rhs=reps_t2[:], start=True, stop=False)
+            nc.tensor.matmul(bank[:, 0:P], lhsT=e2t[:, cols], rhs=ones_f[:], start=False, stop=True)
+            d2 = tail.tile([P, C], F32, tag="d2t", name="d2t%d" % i, bufs=4)
+            nc.vector.tensor_tensor(out=d2[:], in0=bank[:, 0:P], in1=rr[:], op=ALU.add)
+            nc.vector.tensor_scalar_max(out=d2[:], in0=d2[:], scalar1=0.0)
+            nc.scalar.activation(out=d2[:], in_=d2[:], func=ACT.Sqrt)
+            roots.append(d2)
+            if i >= 1:
+                nc.vector.tensor_scalar_mul(out=o[:, i - 1, :], in0=roots[i - 1][:], scalar1=-1.0)
+        nc.sync.dma_start(out=out_v[:, 4:7, :], in_=o[:, 0:3, :])
+        nc.vector.tensor_scalar_mul(out=o[:, 3, :], in0=roots[3][:], scalar1=-1.0)
+        nc.sync.dma_start(out=out_v[:, 7:8, :], in_=o[:, 3:4, :])

@@ -21,7 +21,6 @@ RING = 6
 def tile_minerva_detex_pb_kernel(tc, f_n, ex_n, ex_classes, class_reps, out):
     nc = tc.nc
     with ExitStack() as ctx:
-        ctx.enter_context(tc.manual_schedule())
         const = ctx.enter_context(tc.tile_pool(name="const", bufs=1))
         loads = ctx.enter_context(tc.tile_pool(name="loads", bufs=1))
         keep = ctx.enter_context(tc.tile_pool(name="keep", bufs=1))

@@ -21,6 +21,7 @@ RING = 6
 def tile_minerva_detex_pb_kernel(tc, f_n, ex_n, ex_classes, class_reps, out):
     nc = tc.nc
     with ExitStack() as ctx:
+        ctx.enter_context(tc.manual_schedule())
         const = ctx.enter_context(tc.tile_pool(name="const", bufs=1))
         loads = ctx.enter_context(tc.tile_pool(name="loads", bufs=1))
         keep = ctx.enter_context(tc.tile_pool(name="keep", bufs=1))
@@ -38,6 +39,10 @@ def tile_minerva_detex_pb_kernel(tc, f_n, ex_n, ex_classes, class_reps, out):
         exc_v = ex_classes.rearrange("(g p j) c -> p g j c", p=P, j=4)
         out_v = out.rearrange("(p t) k -> p t k", t=8)
 
+        idle_w = const.tile([P, P], BF16, name="idle_w")
+        nc.vector.memset(idle_w[:], 0.0)
+        idle_x = const.tile([P, 512], BF16, name="idle_x")
+        nc.vector.memset(idle_x[:], 0.0)
         ident_f = const.tile([P, P], F32, name="ident_f")
         make_identity(nc, ident_f[:])
         ident_b = const.tile([P, P], BF16, name="ident_b")
@@ -83,6 +88,11 @@ def tile_minerva_detex_pb_kernel(tc, f_n, ex_n, ex_classes, class_reps, out):
             banks.append(bank)
             return bank
 
+        def keep_clock_up(columns):
+            nc.tensor.matmul(
+                echo[1][:, 0:columns], lhsT=idle_w[:], rhs=idle_x[:, 0:columns], start=True, stop=True
+            )
+
         def copy_out(engine, out_ap, in_ap):
             if engine == "scalar":
                 nc.scalar.copy(out=out_ap, in_=in_ap)
@@ -94,6 +104,8 @@ def tile_minerva_detex_pb_kernel(tc, f_n, ex_n, ex_classes, class_reps, out):
             words = rows.bitcast(F32)
             for i in range(4):
                 nc.tensor.transpose(bank[:, i * P : (i + 1) * P], words[:, i * P : (i + 1) * P], ident_f[:])
+            if len(banks) <= 8:
+                keep_clock_up(256)
             copy_out(
                 engine,
                 dst.bitcast(F32).rearrange("p (kp r u) -> p kp r u", kp=2, u=2),
@@ -281,6 +293,8 @@ def tile_minerva_detex_pb_kernel(tc, f_n, ex_n, ex_classes, class_reps, out):
             nc.sync.dma_start(out=out_v[:, 4 * h : 4 * h + 4, :], in_=o_tiles[h][:])
 
         both_scalar = ("scalar", "scalar")
+        for i in range(8):
+            keep_clock_up(512)
         ex_pair(0, both_scalar)
         quantise_ex_pair(0)
         ex_pair(1, both_scalar)

@@ -39,8 +39,6 @@ def tile_minerva_detex_pb_kernel(tc, f_n, ex_n, ex_classes, class_reps, out):
         exc_v = ex_classes.rearrange("(g p j) c -> p g j c", p=P, j=4)
         out_v = out.rearrange("(p t) k -> p t k", t=8)
 
-        idle_w = const.tile([P, P], BF16, name="idle_w")
-        nc.vector.memset(idle_w[:], 0.0)
         idle_x = const.tile([P, 512], BF16, name="idle_x")
         nc.vector.memset(idle_x[:], 0.0)
         ident_f = const.tile([P, P], F32, name="ident_f")
@@ -90,7 +88,7 @@ def tile_minerva_detex_pb_kernel(tc, f_n, ex_n, ex_classes, class_reps, out):
 
         def keep_clock_up(columns):
             nc.tensor.matmul(
-                echo[1][:, 0:columns], lhsT=idle_w[:], rhs=idle_x[:, 0:columns], start=True, stop=True
+                echo[1][:, 0:columns], lhsT=idle_x[:, 0:P], rhs=idle_x[:, 0:columns], start=True, stop=True
             )
 
         def copy_out(engine, out_ap, in_ap):
@@ -293,7 +291,7 @@ def tile_minerva_detex_pb_kernel(tc, f_n, ex_n, ex_classes, class_reps, out):
             nc.sync.dma_start(out=out_v[:, 4 * h : 4 * h + 4, :], in_=o_tiles[h][:])
 
         both_scalar = ("scalar", "scalar")
-        for i in range(8):
+        for i in range(4):
             keep_clock_up(512)
         ex_pair(0, both_scalar)
         quantise_ex_pair(0)

from contextlib import ExitStack

import concourse.mybir as mybir
from concourse.masks import make_identity

F32 = mybir.dt.float32
BF16 = mybir.dt.bfloat16
U32 = mybir.dt.uint32
U8 = mybir.dt.uint8
FP8X4 = mybir.dt.float8_e4m3fn_x4
ACT = mybir.ActivationFunctionType
ALU = mybir.AluOpType

P = 128
B, D, F, C = 1024, 4096, 1024, 128
FLOPS = 2 * B * D * F + 2 * D * C * C + 2 * B * D * C + 4 * B * C * C

RING = 6


def tile_minerva_detex_pb_kernel(tc, f_n, ex_n, ex_classes, class_reps, out):
    nc = tc.nc
    with ExitStack() as ctx:
        ctx.enter_context(tc.manual_schedule())
        const = ctx.enter_context(tc.tile_pool(name="const", bufs=1))
        loads = ctx.enter_context(tc.tile_pool(name="loads", bufs=1))
        keep = ctx.enter_context(tc.tile_pool(name="keep", bufs=1))
        grouped_pool = ctx.enter_context(tc.tile_pool(name="grouped", bufs=4))
        xcodes_pool = ctx.enter_context(tc.tile_pool(name="xcodes", bufs=3))
        sq_pool = ctx.enter_context(tc.tile_pool(name="sq", bufs=3))
        a_pool = ctx.enter_context(tc.tile_pool(name="a", bufs=3))
        acodes_pool = ctx.enter_context(tc.tile_pool(name="acodes", bufs=6))
        c_pool = ctx.enter_context(tc.tile_pool(name="c", bufs=3))
        tail = ctx.enter_context(tc.tile_pool(name="tail", bufs=2))
        psum = ctx.enter_context(tc.psum_pool(name="psum", bufs=1))

        ex_v = ex_n.rearrange("(g p j) f -> p g j f", p=P, j=4)
        f_v = f_n.rearrange("(p t) f -> p t f", t=8)
        exc_v = ex_classes.rearrange("(g p j) c -> p g j c", p=P, j=4)
        out_v = out.rearrange("(p t) k -> p t k", t=8)

        idle_x = const.tile([P, 512], BF16, name="idle_x")
        nc.vector.memset(idle_x[:], 0.0)
        ident_f = const.tile([P, P], F32, name="ident_f")
        make_identity(nc, ident_f[:])
        ident_b = const.tile([P, P], BF16, name="ident_b")
        make_identity(nc, ident_b[:])
        warm = const.tile([P, 1], F32, name="warm")
        nc.vector.memset(warm[:], 1.0)
        warm_out = const.tile([P, 1], F32, name="warm_out")
        nc.scalar.activation(out=warm_out[:], in_=warm[:], func=ACT.Sqrt)
        ones_f = const.tile([P, P], F32, name="ones_f")
        nc.vector.memset(ones_f[:], 1.0)

        ex_rows = {}
        for j in range(4):
            t = loads.tile([P, F], BF16, name="ex0_%d" % j)
            nc.sync.dma_start(out=t[:], in_=ex_v[:, 0, j, :])
            ex_rows[(0, j)] = t[:]
        f_rows = {}
        for bt in range(4):
            t = loads.tile([P, F], BF16, name="f_%d" % bt)
            nc.sync.dma_start(out=t[:], in_=f_v[:, bt, :])
            f_rows[bt] = t[:]
        f_hi = loads.tile([P, 4, F], BF16, name="f_hi")
        nc.sync.dma_start(out=f_hi[:], in_=f_v[:, 4:8, :])
        for bt in range(4, 8):
            f_rows[bt] = f_hi[:, bt - 4, :]
        reps = const.tile([P, C], BF16, name="reps")
        exc_sb = loads.tile([P, 8, 4, C], BF16, name="exc_sb")
        for g in range(1, 8):
            t = loads.tile([P, 4, F], BF16, name="ex%d" % g)
            nc.sync.dma_start(out=t[:], in_=ex_v[:, g, :, :])
            for j in range(4):
                ex_rows[(g, j)] = t[:, j, :]
            if g == 2:
                nc.sync.dma_start(out=reps[:], in_=class_reps)
                nc.sync.dma_start(out=exc_sb[:], in_=exc_v)

        echo = [psum.tile([P, 512], F32, name="echo%d" % h) for h in range(2)]
        banks = []

        def ring_bank(dtype):
            i = len(banks)
            bank = psum.tile([P, 512], dtype, tag="ring%d" % (i % RING), name="bank%d" % i)
            banks.append(bank)
            return bank

        def keep_clock_up(columns):
            nc.tensor.matmul(
                echo[1][:, 0:columns], lhsT=idle_x[:, 0:P], rhs=idle_x[:, 0:columns], start=True, stop=True
            )

        def copy_out(engine, out_ap, in_ap):
            if engine == "scalar":
                nc.scalar.copy(out=out_ap, in_=in_ap)
            else:
                nc.vector.tensor_copy(out=out_ap, in_=in_ap)

        def transpose_rows(rows, dst, engine):
            bank = ring_bank(F32)
            words = rows.bitcast(F32)
            for i in range(4):
                nc.tensor.transpose(bank[:, i * P : (i + 1) * P], words[:, i * P : (i + 1) * P], ident_f[:])
            if len(banks) <= 8:
                keep_clock_up(256)
            copy_out(
                engine,
                dst.bitcast(F32).rearrange("p (kp r u) -> p kp r u", kp=2, u=2),
                bank[:].rearrange("p (kp u r) -> p kp r u", kp=2, u=2),
            )

        def quantise(src, codes, scales):
            nc.vector.quantize_mx(out=codes.bitcast(FP8X4), scales=scales, in_=src)

        ex_codes = {}
        pair_tiles = {}

        def ex_pair(v, engines):
            g, hh = divmod(v, 2)
            grp = grouped_pool.tile([P, 2, F], BF16, tag="grouped", name="xg%d" % v, align_bytes=64)
            for jj in range(2):
                transpose_rows(ex_rows[(g, 2 * hh + jj)], grp[:, jj, :], engines[jj])
            pair_tiles[v] = grp

        def quantise_ex_pair(v):
            g, hh = divmod(v, 2)
            if hh == 0:
                xc = xcodes_pool.tile([P, 1024], U32, tag="xc", name="xc%d" % g, align_bytes=64)
                xs = xcodes_pool.tile([P, 1024], U8, tag="xs", name="xs%d" % g, align_bytes=64)
                ex_codes[g] = (xc, xs)
            xc, xs = ex_codes[g]
            cols = slice(hh * 512, (hh + 1) * 512)
            quantise(pair_tiles[v][:].rearrange("p a b -> p (a b)"), xc[:, cols], xs[:, cols])

        f_codes = {}

        f_tiles = {}

        def f_transpose(bt, engine):
            fg = grouped_pool.tile([P, F], BF16, tag="fgrouped", name="fg%d" % bt, align_bytes=64)
            transpose_rows(f_rows[bt], fg[:], engine)
            f_tiles[bt] = fg

        def quantise_f(bt):
            fc = keep.tile([P, 256], U32, name="fc%d" % bt, align_bytes=64)
            fs = keep.tile([P, 256], U8, name="fs%d" % bt, align_bytes=64)
            f_codes[bt] = (fc, fs)
            quantise(f_tiles[bt][:], fc[:], fs[:])

        a_tiles = {}
        a_codes = {}

        def s_bank(n):
            g, bt = divmod(n, 8)
            u, i = divmod(n, 4)
            bank = ring_bank(F32)
            xc, xs = ex_codes[g]
            fc, fs = f_codes[bt]
            for j in range(4):
                for kp in range(2):
                    lc = slice((2 * j + kp) * P, (2 * j + kp + 1) * P)
                    rc = slice(kp * P, (kp + 1) * P)
                    nc.tensor.matmul_mx(
                        out=bank[:, j * P : (j + 1) * P],
                        lhsT=xc[:, lc].bitcast(FP8X4),
                        lhsT_scale=xs[:, lc],
                        rhs=fc[:, rc].bitcast(FP8X4),
                        rhs_scale=fs[:, rc],
                        start=(kp == 0),
                        stop=(kp == 1),
                    )
            by_query = bank[:].rearrange("p (j b) -> p b j", j=4)
            sq = sq_pool.tile([P, P, 4], F32, tag="sq", name="sq%d" % n)
            nc.scalar.activation(out=sq[:], in_=by_query, func=ACT.Square)
            if i == 0:
                a_tiles[u] = a_pool.tile([P, 4, P, 4], BF16, tag="a", name="a%d" % u, align_bytes=64)
            nc.vector.tensor_tensor(out=a_tiles[u][:, i, :, :], in0=sq[:], in1=by_query, op=ALU.mult)

        def quantise_a(u):
            ac = acodes_pool.tile([P, 512], U32, tag="ac", name="ac%d" % u, align_bytes=64)
            asc = acodes_pool.tile([P, 512], U8, tag="as", name="as%d" % u, align_bytes=64)
            a_codes[u] = (ac, asc)
            quantise(a_tiles[u][:].rearrange("p i b j -> p (i b j)"), ac[:], asc[:])

        ct_tiles = {}
        cg_tiles = {}
        c_codes = {}

        def classes_transpose(g):
            bank = ring_bank(BF16)
            for j in range(4):
                nc.tensor.transpose(bank[:, j * P : (j + 1) * P], exc_sb[:, g, j, :], ident_b[:])
            ct = c_pool.tile([P, 512], BF16, tag="ct", name="ct%d" % g)
            nc.scalar.copy(out=ct[:], in_=bank[:])
            ct_tiles[g] = ct

        def class_reps_of_exemplars(g):
            bank = ring_bank(F32)
            for j in range(4):
                nc.tensor.matmul(
                    bank[:, j * P : (j + 1) * P],
                    lhsT=ct_tiles[g][:, j * P : (j + 1) * P],
                    rhs=reps[:],
                    start=True,
                    stop=True,
                )
            cg = c_pool.tile([P, 512], BF16, tag="cg", name="cg%d" % g, align_bytes=64)
            nc.scalar.copy(
                out=cg[:].rearrange("p (c j) -> p c j", j=4), in_=bank[:].rearrange("p (j c) -> p c j", j=4)
            )
            cg_tiles[g] = cg

        def quantise_class_reps(g):
            cc = keep.tile([P, P], U32, name="cc%d" % g, align_bytes=64)
            cs = keep.tile([P, P], U8, name="cs%d" % g, align_bytes=64)
            c_codes[g] = (cc, cs)
            quantise(cg_tiles[g][:], cc[:], cs[:])

        def echo_pass(u):
            g, h = divmod(u, 2)
            cc, cs = c_codes[g]
            ac, asc = a_codes[u]
            nc.tensor.matmul_mx(
                out=echo[h][:],
                lhsT=cc[:].bitcast(FP8X4),
                lhsT_scale=cs[:],
                rhs=ac[:].bitcast(FP8X4),
                rhs_scale=asc[:],
                start=(g == 0),
                stop=(g == 7),
            )

        reps_t2 = const.tile([P, C], F32, name="reps_t2")
        reps_tsq = const.tile([P, C], F32, name="reps_tsq")
        rr = const.tile([P, C], F32, name="rr")

        def reps_transpose():
            bank = ring_bank(BF16)
            nc.tensor.transpose(bank[:, 0:P], reps[:], ident_b[:])
            nc.scalar.mul(out=reps_t2[:], in_=bank[:, 0:P], mul=-2.0)
            nc.scalar.activation(out=reps_tsq[:], in_=bank[:, 0:P], func=ACT.Square)

        def reps_norms():
            bank = ring_bank(F32)
            nc.tensor.matmul(bank[:, 0:P], lhsT=ones_f[:], rhs=reps_tsq[:], start=True, stop=True)
            nc.vector.tensor_copy(out=rr[:], in_=bank[:, 0:P])

        e_tiles = {}
        d_banks = {}
        d2_tiles = {}
        o_tiles = {}

        def echo_out(h):
            et = tail.tile([P, 512], F32, tag="et", name="et%d" % h)
            e2t = tail.tile([P, 512], F32, tag="e2t", name="e2t%d" % h)
            for i in range(4):
                cols = slice(i * P, (i + 1) * P)
                nc.scalar.copy(out=et[:, cols], in_=echo[h][:, cols])
                nc.scalar.activation(out=e2t[:, cols], in_=echo[h][:, cols], func=ACT.Square)
            e_tiles[h] = (et, e2t)
            o_tiles[h] = tail.tile([P, 4, C], F32, tag="o", name="o%d" % h)

        def distance_products(h, c):
            et, e2t = e_tiles[h]
            bank = ring_bank(F32)
            for i2 in range(2):
                cols = slice((2 * c + i2) * P, (2 * c + i2 + 1) * P)
                dst = bank[:, i2 * P : (i2 + 1) * P]
                nc.tensor.matmul(dst, lhsT=et[:, cols], rhs=reps_t2[:], start=True, stop=False)
                nc.tensor.matmul(dst, lhsT=e2t[:, cols], rhs=ones_f[:], start=False, stop=True)
            d_banks[(h, c)] = bank

        def distance_sum(h, c):
            d2 = tail.tile([P, 2, C], F32, tag="d2", name="d2_%d%d" % (h, c))
            nc.vector.tensor_tensor(
                out=d2[:],
                in0=d_banks[(h, c)][:, 0 : 2 * P].rearrange("p (i k) -> p i k", i=2),
                in1=rr[:].unsqueeze(1).to_broadcast([P, 2, C]),
                op=ALU.add,
            )
            d2_tiles[(h, c)] = d2

        def distance_root(h, c):
            d2 = d2_tiles[(h, c)]
            nc.scalar.activation(out=d2[:], in_=d2[:], func=ACT.Relu)
            nc.scalar.activation(out=d2[:], in_=d2[:], func=ACT.Sqrt)
            nc.scalar.mul(out=o_tiles[h][:, 2 * c : 2 * c + 2, :], in_=d2[:], mul=-1.0)

        def store(h):
            nc.sync.dma_start(out=out_v[:, 4 * h : 4 * h + 4, :], in_=o_tiles[h][:])

        both_scalar = ("scalar", "scalar")
        for i in range(4):
            keep_clock_up(512)
        ex_pair(0, both_scalar)
        quantise_ex_pair(0)
        ex_pair(1, both_scalar)
        quantise_ex_pair(1)
        for bt in range(4):
            f_transpose(bt, "scalar")
            quantise_f(bt)
        quantised = [2]
        for u in range(16):
            g, h = divmod(u, 2)
            if u == 2:
                ex_pair(4, ("scalar", "vector"))
                ex_pair(5, ("scalar", "vector"))
            elif u >= 3 and u + 3 < 16:
                ex_pair(u + 3, both_scalar)
            if u == 3:
                classes_transpose(0)
                classes_transpose(1)
                reps_transpose()
            if h == 1 and u >= 3 and g + 1 < 8:
                classes_transpose(g + 1)
            if u >= 3:
                for v in range(quantised[0], min(u + 3, 16)):
                    quantise_ex_pair(v)
                quantised[0] = min(u + 3, 16)
            if u >= 1:
                quantise_a(u - 1)
            if h == 0 and g >= 2:
                quantise_class_reps(g)
            for i in range(4):
                n = 4 * u + i
                if n == 3:
                    for bt in range(4, 8):
                        f_transpose(bt, ("scalar", "vector")[bt % 2])
                    for bt in range(4, 8):
                        quantise_f(bt)
                if n == 4:
                    ex_pair(2, both_scalar)
                if n == 6:
                    ex_pair(3, both_scalar)
                    quantise_ex_pair(2)
                    quantise_ex_pair(3)
                    quantised[0] = 4
                if n == 17:
                    class_reps_of_exemplars(0)
                    class_reps_of_exemplars(1)
                    reps_norms()
                    quantise_class_reps(0)
                    quantise_class_reps(1)
                if i == 1:
                    if u == 5:
                        for uu in range(4):
                            echo_pass(uu)
                    elif u > 5:
                        echo_pass(u - 2)
                s_bank(n)
            if h == 1 and u >= 3 and g + 1 < 8:
                class_reps_of_exemplars(g + 1)
        echo_pass(14)
        echo_out(0)
        distance_products(0, 0)
        distance_products(0, 1)
        distance_sum(0, 0)
        quantise_a(15)
        echo_pass(15)
        distance_root(0, 0)
        distance_sum(0, 1)
        et = tail.tile([P, 512], F32, tag="et", name="et1")
        e2t = tail.tile([P, 512], F32, tag="e2t", name="e2t1")
        o = tail.tile([P, 4, C], F32, tag="o", name="o1")
        for i in range(4):
            cols = slice(i * P, (i + 1) * P)
            nc.scalar.copy(out=et[:, cols], in_=echo[1][:, cols])
            nc.vector.tensor_tensor(out=e2t[:, cols], in0=et[:, cols], in1=et[:, cols], op=ALU.mult)
        distance_root(0, 1)
        store(0)
        roots = []
        for i in range(4):
            cols = slice(i * P, (i + 1) * P)
            bank = ring_bank(F32)
            nc.tensor.matmul(bank[:, 0:P], lhsT=et[:, cols], rhs=reps_t2[:], start=True, stop=False)
            nc.tensor.matmul(bank[:, 0:P], lhsT=e2t[:, cols], rhs=ones_f[:], start=False, stop=True)
            d2 = tail.tile([P, C], F32, tag="d2t", name="d2t%d" % i, bufs=4)
            nc.vector.tensor_tensor(out=d2[:], in0=bank[:, 0:P], in1=rr[:], op=ALU.add)
            nc.vector.tensor_scalar_max(out=d2[:], in0=d2[:], scalar1=0.0)
            nc.scalar.activation(out=d2[:], in_=d2[:], func=ACT.Sqrt)
            roots.append(d2)
            if i >= 1:
                nc.vector.tensor_scalar_mul(out=o[:, i - 1, :], in0=roots[i - 1][:], scalar1=-1.0)
        nc.sync.dma_start(out=out_v[:, 4:7, :], in_=o[:, 0:3, :])
        nc.vector.tensor_scalar_mul(out=o[:, 3, :], in0=roots[3][:], scalar1=-1.0)
        nc.sync.dma_start(out=out_v[:, 7:8, :], in_=o[:, 3:4, :])
